import numpy as np
import ml_dtypes


def mxq(x, axis, fmt="e4m3"):
    dtype, down = {"e4m3": (ml_dtypes.float8_e4m3fn, 7), "e5m2": (ml_dtypes.float8_e5m2, 14)}[fmt]
    v = np.moveaxis(np.asarray(x, np.float32).astype(ml_dtypes.bfloat16).astype(np.float64), axis, -1)
    blocks = v.reshape(v.shape[:-1] + (-1, 32))
    amax = np.abs(blocks).max(-1, keepdims=True)
    byte = np.maximum(np.where(amax > 0, np.frexp(amax)[1] - 1 + 127, 0) - down, 1)
    scale = np.exp2(byte - 127.0)
    codes = (blocks / scale).astype(np.float32).astype(dtype).astype(np.float64)
    return np.moveaxis((codes * scale).reshape(v.shape), -1, axis)


WIDE = False


def mx_kscale(k):
    if not WIDE:
        return np.ones(k)
    levels = np.array([10, -10, 5, -5, 0])
    a = np.random.permutation(np.resize(levels, k // 512 * 4)).reshape(k // 512, 4)
    idx = np.arange(k)
    return np.exp2(a[idx // 512, idx % 128 // 32])


BF16 = ml_dtypes.bfloat16


def bf(x):
    return np.asarray(x, np.float32).astype(BF16)


def f64(x):
    return np.asarray(x).astype(np.float64)


B, CIN, COUT, E, G, NC = 8192, 512, 256, 4, 2, 2
OMEGA_0 = 30.0


def setup_inputs():
    s = mx_kscale(CIN)
    wb = np.sqrt(6.0 / CIN) / OMEGA_0
    return {"in_feats": bf(np.random.standard_normal((B, CIN)) * s),
            "tile_gate": bf(np.random.standard_normal((B, E)) / np.sqrt(E)),
            "W": bf(np.random.uniform(-wb, wb, (E, COUT, CIN)) / s)}


def reference(in_feats, tile_gate, W):
    xq = mxq(f64(in_feats), 1, "e4m3")
    wq = mxq(f64(W), 2, "e4m3")
    g = f64(tile_gate)
    out = np.zeros((B, COUT))
    for t in range(E):
        out = out + g[:, t:t + 1] * (xq @ wq[t].T)
    return np.sin(OMEGA_0 * out)

@@ -1,0 +1,208 @@
+import math
+from contextlib import ExitStack
+
+import concourse.mybir as mybir
+from concourse.masks import make_identity
+
+F32 = mybir.dt.float32
+BF16 = mybir.dt.bfloat16
+I32 = mybir.dt.int32
+U32 = mybir.dt.uint32
+U8 = mybir.dt.uint8
+FP8X4 = mybir.dt.float8_e4m3fn_x4
+ALU = mybir.AluOpType
+ACT = mybir.ActivationFunctionType
+
+P = 128
+B, CIN, COUT, E = 8192, 512, 256, 4
+NT = B // P
+GT = 4
+NG = NT // GT
+FLOPS = 2 * B * CIN * COUT * E
+
+MANUAL = False
+TWO = (False, True, False, True)
+EXIT_ENG = ("s", "s")
+CAST_ENG = "g"
+
+
+def tile_sinelayer_loe_pa_t_kernel(tc, in_feats, tile_gate, W, out):
+    nc = tc.nc
+    x_v = in_feats.rearrange("(p r) k -> p (r k)", p=P)
+    g_v = tile_gate.rearrange("(p r) e -> p (r e)", p=P)
+    w_v = W.rearrange("t (h p) k -> p (t h) k", p=P)
+    o_v = out.rearrange("(p r) c -> p (r c)", p=P)
+
+    with ExitStack() as ctx:
+        if MANUAL:
+            ctx.enter_context(tc.manual_schedule())
+        const = ctx.enter_context(tc.tile_pool(name="const", bufs=1))
+        gpool = ctx.enter_context(tc.tile_pool(name="gpool", bufs=3))
+        spool = ctx.enter_context(tc.tile_pool(name="spool", bufs=4))
+        rpool = ctx.enter_context(tc.tile_pool(name="rpool", bufs=3))
+        psx = ctx.enter_context(tc.psum_pool(name="psx", bufs=2))
+        psp = ctx.enter_context(tc.psum_pool(name="psp", bufs=3))
+
+        w_sb = const.tile([P, 8 * CIN], BF16, name="w_sb")
+        w_sb3 = w_sb[:].rearrange("p (a k) -> p a k", a=8)
+        for q in range(4):
+            nc.sync.dma_start(out=w_sb3[:, 2 * q:2 * q + 2, :], in_=w_v[:, 2 * q:2 * q + 2, :])
+        gate_sb = const.tile([P, NT * E], BF16, name="gate_sb")
+        nc.scalar.dma_start(out=gate_sb[:], in_=g_v)
+        xs = []
+        for g in range(NG):
+            x_t = const.tile([P, GT * CIN], BF16, name="x%d" % g)
+            nc.sync.dma_start(out=x_t[:], in_=x_v[:, g * GT * CIN:(g + 1) * GT * CIN])
+            xs.append(x_t)
+
+        ident = const.tile([P, P], F32, name="ident")
+        make_identity(nc, ident[:])
+        zero = const.tile([P, 1], F32, name="zero")
+        nc.vector.memset(zero[:], 0.0)
+        warm = const.tile([P, 1], F32, name="warm")
+        nc.scalar.activation(out=warm[:], in_=zero[:], func=ACT.Sin)
+        gs = const.tile([P, NT * E], F32, name="gs")
+        nc.vector.tensor_scalar(out=gs[:], in0=gate_sb[:], scalar1=30.0 / (2.0 * math.pi),
+                                scalar2=None, op0=ALU.mult)
+
+        def copy_out(eng, dst, src):
+            if eng == "s":
+                nc.scalar.copy(out=dst, in_=src)
+            else:
+                nc.vector.tensor_copy(out=dst, in_=src)
+
+        def transposes(bank, src_f32, first):
+            for jj in range(2):
+                for u in range(2):
+                    c = (first + jj) * 256 + u * P
+                    nc.tensor.transpose(bank[:, (jj * 2 + u) * P:(jj * 2 + u + 1) * P],
+                                        src_f32[:, c:c + P], ident[:])
+
+        def regroup(eng, grp_f32, h, bank):
+            copy_out(eng,
+                     grp_f32[:, h * 512:(h + 1) * 512].rearrange("p (j m u) -> p j m u", j=2, u=2),
+                     bank[:].rearrange("p (j u m) -> p j m u", j=2, u=2))
+
+        w_f32 = w_sb[:].bitcast(F32)
+        w_grp = const.tile([P, 8 * CIN], BF16, name="w_grp", align_bytes=64)
+        w_grp_f32 = w_grp[:].bitcast(F32)
+        w_codes = const.tile([P, E * COUT], U32, name="w_codes", align_bytes=64)
+        w_scl = const.tile([P, E * COUT], U8, name="w_scl", align_bytes=64)
+        for q in range(4):
+            wt = psp.tile([P, 512], F32, tag=("pa" if q % 2 == 0 else "pb"), name="wt%d" % q)
+            transposes(wt, w_f32, 2 * q)
+            regroup("s" if q % 2 == 0 else "v", w_grp_f32, q, wt)
+        for h in range(2):
+            nc.vector.quantize_mx(out=w_codes[:, h * 512:(h + 1) * 512].bitcast(FP8X4),
+                                  scales=w_scl[:, h * 512:(h + 1) * 512],
+                                  in_=w_grp[:, h * 2048:(h + 1) * 2048])
+
+        grp = {}
+        banks = {}
+        codes = {}
+        scl = {}
+        u_t = {}
+        o_t = {}
+        k_t = {}
+        r_t = {}
+
+        def stage_t(g):
+            grp[g] = gpool.tile([P, GT * CIN], BF16, tag="grp", name="grp%d" % g, align_bytes=64)
+            xf = xs[g][:].bitcast(F32)
+            for h in range(2):
+                bank = psx.tile([P, 512], F32, tag="xt", name="xt%d_%d" % (g, h))
+                transposes(bank, xf, 2 * h)
+                banks[(g, h)] = bank
+
+        def stage_exit(g, h):
+            regroup(EXIT_ENG[h], grp[g][:].bitcast(F32), h, banks[(g, h)])
+
+        def stage_q(g):
+            codes[g] = gpool.tile([P, GT * P], U32, tag="codes", name="codes%d" % g, align_bytes=64)
+            scl[g] = gpool.tile([P, GT * P], U8, tag="scl", name="scl%d" % g, align_bytes=64)
+            nc.vector.quantize_mx(out=codes[g][:].bitcast(FP8X4), scales=scl[g][:], in_=grp[g][:])
+
+        def stage_m(g, jj):
+            if jj == 0:
+                u_t[g] = rpool.tile([P, GT * COUT], F32, tag="u", name="u%d" % g)
+            j = g * GT + jj
+            pa = psp.tile([P, 512], F32, tag="pa", name="pa%d" % j)
+            pb = psp.tile([P, 512], F32, tag="pb", name="pb%d" % j)
+            for h, bank in ((0, pa), (1, pb)):
+                nc.tensor.matmul_mx(out=bank[:],
+                                    lhsT=codes[g][:, jj * P:(jj + 1) * P].bitcast(FP8X4),
+                                    lhsT_scale=scl[g][:, jj * P:(jj + 1) * P],
+                                    rhs=w_codes[:, h * 512:(h + 1) * 512].bitcast(FP8X4),
+                                    rhs_scale=w_scl[:, h * 512:(h + 1) * 512],
+                                    start=True, stop=True)
+
+            def gcol(t):
+                return gs[:, j * E + t:j * E + t + 1]
+
+            def stt(dst, src, t, add):
+                nc.vector.scalar_tensor_tensor(out=dst, in0=src, scalar=gcol(t), in1=add,
+                                               op0=ALU.mult, op1=ALU.add)
+
+            u_dst = u_t[g][:, jj * COUT:(jj + 1) * COUT]
+            sa0 = spool.tile([P, COUT], F32, tag="sa0", name="sa0_%d" % j)
+            nc.scalar.activation(out=sa0[:], in_=pa[:, 0:COUT], func=ACT.Copy, scale=gcol(0))
+            acc = spool.tile([P, COUT], F32, tag="acc", name="acc%d" % j)
+            if TWO[jj]:
+                sa1 = spool.tile([P, COUT], F32, tag="sa1", name="sa1_%d" % j)
+                nc.scalar.activation(out=sa1[:], in_=pa[:, COUT:2 * COUT], func=ACT.Copy, scale=gcol(1))
+                a01 = spool.tile([P, COUT], F32, tag="a01", name="a01_%d" % j)
+                nc.gpsimd.tensor_tensor(out=a01[:], in0=sa0[:], in1=sa1[:], op=ALU.add)
+                stt(acc[:], pb[:, 0:COUT], 2, a01[:])
+            else:
+                acc1 = spool.tile([P, COUT], F32, tag="acc1", name="acc1_%d" % j)
+                stt(acc1[:], pa[:, COUT:2 * COUT], 1, sa0[:])
+                stt(acc[:], pb[:, 0:COUT], 2, acc1[:])
+            stt(u_dst, pb[:, COUT:2 * COUT], 3, acc[:])
+
+        def stage_cast(g, h):
+            k_t[(g, h)] = rpool.tile([P, 512], I32, tag="k", name="k%d_%d" % (g, h))
+            src = u_t[g][:, h * 512:(h + 1) * 512]
+            if CAST_ENG == "g":
+                nc.gpsimd.tensor_scalar(out=k_t[(g, h)][:], in0=src, scalar1=1.0, scalar2=0.0,
+                                        op0=ALU.mult, op1=ALU.add)
+            else:
+                nc.vector.tensor_copy(out=k_t[(g, h)][:], in_=src)
+
+        def stage_sub(g, h):
+            r_t[(g, h)] = rpool.tile([P, 512], F32, tag="r", name="r%d_%d" % (g, h))
+            nc.vector.tensor_tensor(out=r_t[(g, h)][:], in0=u_t[g][:, h * 512:(h + 1) * 512],
+                                    in1=k_t[(g, h)][:], op=ALU.subtract)
+
+        def stage_sin(g, h):
+            if h == 0:
+                o_t[g] = rpool.tile([P, GT * COUT], F32, tag="o", name="o%d" % g)
+            nc.scalar.activation(out=o_t[g][:, h * 512:(h + 1) * 512], in_=r_t[(g, h)][:],
+                                 func=ACT.Sin, scale=2.0 * math.pi)
+            if h == 1:
+                nc.sync.dma_start(out=o_v[:, g * GT * COUT:(g + 1) * GT * COUT], in_=o_t[g][:])
+
+        for i in range(-2, NG + 1):
+            tg, qg, mg, rg = i + 2, i + 1, i, i - 1
+            has_t = tg < NG
+            has_q = 0 <= qg < NG
+            has_m = 0 <= mg < NG
+            has_r = 0 <= rg
+            if has_t:
+                stage_t(tg)
+            for s in range(GT):
+                if has_r and s == 0:
+                    stage_cast(rg, 0)
+                if has_m:
+                    stage_m(mg, s)
+                if has_r and s == 1:
+                    stage_cast(rg, 1)
+                if has_r and s == 0:
+                    stage_sub(rg, 0)
+                if has_q and s == 1:
+                    stage_q(qg)
+                if has_r and s == 2:
+                    stage_sub(rg, 1)
+                if has_t and s < 2:
+                    stage_exit(tg, s)
+                if has_r and s >= 2:
+                    stage_sin(rg, s - 2)

@@ -18,12 +18,12 @@ B, CIN, COUT, E = 8192, 512, 256, 4
 NT = B // P
 GT = 4
 NG = NT // GT
+GW = GT * COUT
 FLOPS = 2 * B * CIN * COUT * E
 
 MANUAL = False
-TWO = (False, True, False, True)
+NTWO = (2,) * 15 + (0,)
 EXIT_ENG = ("s", "s")
-CAST_ENG = "g"
 
 
 def tile_sinelayer_loe_pa_t_kernel(tc, in_feats, tile_gate, W, out):
@@ -32,16 +32,21 @@ def tile_sinelayer_loe_pa_t_kernel(tc, in_feats, tile_gate, W, out):
     g_v = tile_gate.rearrange("(p r) e -> p (r e)", p=P)
     w_v = W.rearrange("t (h p) k -> p (t h) k", p=P)
     o_v = out.rearrange("(p r) c -> p (r c)", p=P)
+    last = NG - 1
 
     with ExitStack() as ctx:
         if MANUAL:
             ctx.enter_context(tc.manual_schedule())
         const = ctx.enter_context(tc.tile_pool(name="const", bufs=1))
-        gpool = ctx.enter_context(tc.tile_pool(name="gpool", bufs=3))
-        spool = ctx.enter_context(tc.tile_pool(name="spool", bufs=4))
-        rpool = ctx.enter_context(tc.tile_pool(name="rpool", bufs=3))
-        psx = ctx.enter_context(tc.psum_pool(name="psx", bufs=2))
-        psp = ctx.enter_context(tc.psum_pool(name="psp", bufs=3))
+        rings = ctx.enter_context(tc.tile_pool(name="rings", bufs=1))
+        psum = ctx.enter_context(tc.psum_pool(name="psum", bufs=1))
+
+        def ring(pool, base, idx, depth, shape, dtype, align=32):
+            if align == 0:
+                return pool.tile(shape, dtype, tag="%s_s%d" % (base, idx % depth),
+                                 name="%s_%d" % (base, idx))
+            return pool.tile(shape, dtype, tag="%s_s%d" % (base, idx % depth),
+                             name="%s_%d" % (base, idx), align_bytes=align)
 
         w_sb = const.tile([P, 8 * CIN], BF16, name="w_sb")
         w_sb3 = w_sb[:].rearrange("p (a k) -> p a k", a=8)
@@ -89,7 +94,7 @@ def tile_sinelayer_loe_pa_t_kernel(tc, in_feats, tile_gate, W, out):
         w_codes = const.tile([P, E * COUT], U32, name="w_codes", align_bytes=64)
         w_scl = const.tile([P, E * COUT], U8, name="w_scl", align_bytes=64)
         for q in range(4):
-            wt = psp.tile([P, 512], F32, tag=("pa" if q % 2 == 0 else "pb"), name="wt%d" % q)
+            wt = ring(psum, ("pa" if q % 2 == 0 else "pb"), q // 2 + 1, 3, [P, 512], F32, 0)
             transposes(wt, w_f32, 2 * q)
             regroup("s" if q % 2 == 0 else "v", w_grp_f32, q, wt)
         for h in range(2):
@@ -102,15 +107,17 @@ def tile_sinelayer_loe_pa_t_kernel(tc, in_feats, tile_gate, W, out):
         codes = {}
         scl = {}
         u_t = {}
+        a1_t = {}
         o_t = {}
         k_t = {}
-        r_t = {}
+        pab = {}
+        sa0_t = {}
 
         def stage_t(g):
-            grp[g] = gpool.tile([P, GT * CIN], BF16, tag="grp", name="grp%d" % g, align_bytes=64)
+            grp[g] = ring(rings, "grp", g, 3, [P, GT * CIN], BF16, 64)
             xf = xs[g][:].bitcast(F32)
             for h in range(2):
-                bank = psx.tile([P, 512], F32, tag="xt", name="xt%d_%d" % (g, h))
+                bank = ring(psum, "xt", 2 * g + h, 2, [P, 512], F32, 0)
                 transposes(bank, xf, 2 * h)
                 banks[(g, h)] = bank
 
@@ -118,16 +125,27 @@ def tile_sinelayer_loe_pa_t_kernel(tc, in_feats, tile_gate, W, out):
             regroup(EXIT_ENG[h], grp[g][:].bitcast(F32), h, banks[(g, h)])
 
         def stage_q(g):
-            codes[g] = gpool.tile([P, GT * P], U32, tag="codes", name="codes%d" % g, align_bytes=64)
-            scl[g] = gpool.tile([P, GT * P], U8, tag="scl", name="scl%d" % g, align_bytes=64)
+            codes[g] = ring(rings, "codes", g, 3, [P, GT * P], U32, 64)
+            scl[g] = ring(rings, "scl", g, 3, [P, GT * P], U8, 64)
             nc.vector.quantize_mx(out=codes[g][:].bitcast(FP8X4), scales=scl[g][:], in_=grp[g][:])
 
-        def stage_m(g, jj):
+        def gcol(j, t):
+            return gs[:, j * E + t:j * E + t + 1]
+
+        def is_two(g, jj):
+            return jj >= GT - NTWO[g]
+
+        def stage_mm(g, jj):
             if jj == 0:
-                u_t[g] = rpool.tile([P, GT * COUT], F32, tag="u", name="u%d" % g)
+                u_t[g] = ring(rings, "u", g, 4, [P, GW], F32)
+                k_t[g] = ring(rings, "k", g, 4, [P, GW], I32)
+                o_t[g] = ring(rings, "o", g, 5, [P, GW], F32)
+                if NTWO[g] > 0:
+                    a1_t[g] = ring(rings, "a1", g, 4, [P, 3 * COUT], F32)
             j = g * GT + jj
-            pa = psp.tile([P, 512], F32, tag="pa", name="pa%d" % j)
-            pb = psp.tile([P, 512], F32, tag="pb", name="pb%d" % j)
+            pa = ring(psum, "pa", j + 3, 3, [P, 512], F32, 0)
+            pb = ring(psum, "pb", j + 3, 3, [P, 512], F32, 0)
+            pab[j] = (pa, pb)
             for h, bank in ((0, pa), (1, pb)):
                 nc.tensor.matmul_mx(out=bank[:],
                                     lhsT=codes[g][:, jj * P:(jj + 1) * P].bitcast(FP8X4),
@@ -135,74 +153,87 @@ def tile_sinelayer_loe_pa_t_kernel(tc, in_feats, tile_gate, W, out):
                                     rhs=w_codes[:, h * 512:(h + 1) * 512].bitcast(FP8X4),
                                     rhs_scale=w_scl[:, h * 512:(h + 1) * 512],
                                     start=True, stop=True)
+            sa0 = ring(rings, "sa0", j, 6, [P, COUT], F32)
+            sa0_t[j] = sa0
+            nc.scalar.activation(out=sa0[:], in_=pa[:, 0:COUT], func=ACT.Copy, scale=gcol(j, 0))
+            if is_two(g, jj):
+                c = (jj - (GT - NTWO[g])) * COUT
+                nc.scalar.activation(out=a1_t[g][:, c:c + COUT], in_=pa[:, COUT:2 * COUT],
+                                     func=ACT.Copy, scale=gcol(j, 1))
 
-            def gcol(t):
-                return gs[:, j * E + t:j * E + t + 1]
+        def stage_stt(g, jj):
+            j = g * GT + jj
+            pa, pb = pab[j]
 
             def stt(dst, src, t, add):
-                nc.vector.scalar_tensor_tensor(out=dst, in0=src, scalar=gcol(t), in1=add,
+                nc.vector.scalar_tensor_tensor(out=dst, in0=src, scalar=gcol(j, t), in1=add,
                                                op0=ALU.mult, op1=ALU.add)
 
-            u_dst = u_t[g][:, jj * COUT:(jj + 1) * COUT]
-            sa0 = spool.tile([P, COUT], F32, tag="sa0", name="sa0_%d" % j)
-            nc.scalar.activation(out=sa0[:], in_=pa[:, 0:COUT], func=ACT.Copy, scale=gcol(0))
-            acc = spool.tile([P, COUT], F32, tag="acc", name="acc%d" % j)
-            if TWO[jj]:
-                sa1 = spool.tile([P, COUT], F32, tag="sa1", name="sa1_%d" % j)
-                nc.scalar.activation(out=sa1[:], in_=pa[:, COUT:2 * COUT], func=ACT.Copy, scale=gcol(1))
-                a01 = spool.tile([P, COUT], F32, tag="a01", name="a01_%d" % j)
-                nc.gpsimd.tensor_tensor(out=a01[:], in0=sa0[:], in1=sa1[:], op=ALU.add)
-                stt(acc[:], pb[:, 0:COUT], 2, a01[:])
+            acc = ring(rings, "acc", j, 3, [P, COUT], F32)
+            if is_two(g, jj):
+                stt(acc[:], pb[:, 0:COUT], 2, sa0_t[j][:])
             else:
-                acc1 = spool.tile([P, COUT], F32, tag="acc1", name="acc1_%d" % j)
-                stt(acc1[:], pa[:, COUT:2 * COUT], 1, sa0[:])
+                acc1 = ring(rings, "acc1", j, 3, [P, COUT], F32)
+                stt(acc1[:], pa[:, COUT:2 * COUT], 1, sa0_t[j][:])
                 stt(acc[:], pb[:, 0:COUT], 2, acc1[:])
-            stt(u_dst, pb[:, COUT:2 * COUT], 3, acc[:])
+            stt(u_t[g][:, jj * COUT:(jj + 1) * COUT], pb[:, COUT:2 * COUT], 3, acc[:])
 
-        def stage_cast(g, h):
-            k_t[(g, h)] = rpool.tile([P, 512], I32, tag="k", name="k%d_%d" % (g, h))
-            src = u_t[g][:, h * 512:(h + 1) * 512]
-            if CAST_ENG == "g":
-                nc.gpsimd.tensor_scalar(out=k_t[(g, h)][:], in0=src, scalar1=1.0, scalar2=0.0,
-                                        op0=ALU.mult, op1=ALU.add)
-            else:
-                nc.vector.tensor_copy(out=k_t[(g, h)][:], in_=src)
+        def stage_add_cast(g):
+            if NTWO[g] > 0:
+                lo = (GT - NTWO[g]) * COUT
+                nc.gpsimd.tensor_tensor(out=u_t[g][:, lo:GW], in0=u_t[g][:, lo:GW], in1=a1_t[g][:, 0:NTWO[g] * COUT],
+                                        op=ALU.add)
+            nc.gpsimd.tensor_scalar(out=k_t[g][:], in0=u_t[g][:], scalar1=1.0, scalar2=0.0,
+                                    op0=ALU.mult, op1=ALU.add)
 
-        def stage_sub(g, h):
-            r_t[(g, h)] = rpool.tile([P, 512], F32, tag="r", name="r%d_%d" % (g, h))
-            nc.vector.tensor_tensor(out=r_t[(g, h)][:], in0=u_t[g][:, h * 512:(h + 1) * 512],
-                                    in1=k_t[(g, h)][:], op=ALU.subtract)
+        def cast_v(g, lo, hi):
+            nc.vector.tensor_copy(out=k_t[g][:, lo:hi], in_=u_t[g][:, lo:hi])
 
-        def stage_sin(g, h):
-            if h == 0:
-                o_t[g] = rpool.tile([P, GT * COUT], F32, tag="o", name="o%d" % g)
-            nc.scalar.activation(out=o_t[g][:, h * 512:(h + 1) * 512], in_=r_t[(g, h)][:],
-                                 func=ACT.Sin, scale=2.0 * math.pi)
-            if h == 1:
-                nc.sync.dma_start(out=o_v[:, g * GT * COUT:(g + 1) * GT * COUT], in_=o_t[g][:])
+        def sub(g, lo, hi):
+            nc.vector.tensor_tensor(out=u_t[g][:, lo:hi], in0=u_t[g][:, lo:hi], in1=k_t[g][:, lo:hi],
+                                    op=ALU.subtract)
+
+        def sin(g, lo, hi):
+            nc.scalar.activation(out=o_t[g][:, lo:hi], in_=u_t[g][:, lo:hi], func=ACT.Sin,
+                                 scale=2.0 * math.pi)
+
+        def store(g, lo, hi):
+            nc.sync.dma_start(out=o_v[:, g * GW + lo:g * GW + hi], in_=o_t[g][:, lo:hi])
 
         for i in range(-2, NG + 1):
-            tg, qg, mg, rg = i + 2, i + 1, i, i - 1
+            tg, qg, mg, ag, rg = i + 2, i + 1, i, i - 1, i - 2
             has_t = tg < NG
             has_q = 0 <= qg < NG
             has_m = 0 <= mg < NG
-            has_r = 0 <= rg
             if has_t:
                 stage_t(tg)
+            if 0 <= ag < last:
+                stage_add_cast(ag)
             for s in range(GT):
-                if has_r and s == 0:
-                    stage_cast(rg, 0)
                 if has_m:
-                    stage_m(mg, s)
-                if has_r and s == 1:
-                    stage_cast(rg, 1)
-                if has_r and s == 0:
-                    stage_sub(rg, 0)
-                if has_q and s == 1:
-                    stage_q(qg)
-                if has_r and s == 2:
-                    stage_sub(rg, 1)
+                    stage_mm(mg, s)
                 if has_t and s < 2:
                     stage_exit(tg, s)
-                if has_r and s >= 2:
-                    stage_sin(rg, s - 2)
+                if 0 <= rg < last - 1 and s >= 2:
+                    sin(rg, (s - 2) * 512, (s - 1) * 512)
+                    if s == 3:
+                        store(rg, 0, GW)
+                if mg == last and s >= 1:
+                    sin(mg, (s - 1) * COUT, s * COUT)
+                    store(mg, (s - 1) * COUT, s * COUT)
+                if mg == last and s == 3:
+                    sin(last - 1, 0, GW)
+                    store(last - 1, 0, GW)
+                if has_m:
+                    stage_stt(mg, s)
+                if 0 <= rg < last - 1 and s == 0:
+                    sub(rg, 0, GW)
+                if has_q and s == 2:
+                    stage_q(qg)
+                if mg == last:
+                    cast_v(mg, s * COUT, (s + 1) * COUT)
+                    sub(mg, s * COUT, (s + 1) * COUT)
+                    if s == 2:
+                        sub(last - 1, 0, GW)
+        sin(last, 3 * COUT, GW)
+        store(last, 3 * COUT, GW)

@@ -21,9 +21,8 @@ NG = NT // GT
 GW = GT * COUT
 FLOPS = 2 * B * CIN * COUT * E
 
-MANUAL = False
+MANUAL = True
 NTWO = (2,) * 15 + (0,)
-EXIT_ENG = ("s", "s")
 
 
 def tile_sinelayer_loe_pa_t_kernel(tc, in_feats, tile_gate, W, out):
@@ -41,12 +40,13 @@ def tile_sinelayer_loe_pa_t_kernel(tc, in_feats, tile_gate, W, out):
         rings = ctx.enter_context(tc.tile_pool(name="rings", bufs=1))
         psum = ctx.enter_context(tc.psum_pool(name="psum", bufs=1))
 
-        def ring(pool, base, idx, depth, shape, dtype, align=32):
-            if align == 0:
-                return pool.tile(shape, dtype, tag="%s_s%d" % (base, idx % depth),
-                                 name="%s_%d" % (base, idx))
-            return pool.tile(shape, dtype, tag="%s_s%d" % (base, idx % depth),
-                             name="%s_%d" % (base, idx), align_bytes=align)
+        def ring(base, idx, depth, shape, dtype):
+            return rings.tile(shape, dtype, tag="%s_s%d" % (base, idx % depth),
+                              name="%s_%d" % (base, idx), align_bytes=64)
+
+        def bank(base, idx, depth):
+            return psum.tile([P, 512], F32, tag="%s_s%d" % (base, idx % depth),
+                             name="%s_%d" % (base, idx))
 
         w_sb = const.tile([P, 8 * CIN], BF16, name="w_sb")
         w_sb3 = w_sb[:].rearrange("p (a k) -> p a k", a=8)
@@ -70,170 +70,230 @@ def tile_sinelayer_loe_pa_t_kernel(tc, in_feats, tile_gate, W, out):
         nc.vector.tensor_scalar(out=gs[:], in0=gate_sb[:], scalar1=30.0 / (2.0 * math.pi),
                                 scalar2=None, op0=ALU.mult)
 
-        def copy_out(eng, dst, src):
-            if eng == "s":
-                nc.scalar.copy(out=dst, in_=src)
-            else:
-                nc.vector.tensor_copy(out=dst, in_=src)
-
-        def transposes(bank, src_f32, first):
+        def transposes(dst, src_f32, first):
             for jj in range(2):
                 for u in range(2):
                     c = (first + jj) * 256 + u * P
-                    nc.tensor.transpose(bank[:, (jj * 2 + u) * P:(jj * 2 + u + 1) * P],
+                    nc.tensor.transpose(dst[:, (jj * 2 + u) * P:(jj * 2 + u + 1) * P],
                                         src_f32[:, c:c + P], ident[:])
 
-        def regroup(eng, grp_f32, h, bank):
-            copy_out(eng,
-                     grp_f32[:, h * 512:(h + 1) * 512].rearrange("p (j m u) -> p j m u", j=2, u=2),
-                     bank[:].rearrange("p (j u m) -> p j m u", j=2, u=2))
+        def regroup(eng, grp_f32, h, src):
+            dst = grp_f32[:, h * 512:(h + 1) * 512].rearrange("p (j m u) -> p j m u", j=2, u=2)
+            view = src[:].rearrange("p (j u m) -> p j m u", j=2, u=2)
+            if eng == "s":
+                nc.scalar.copy(out=dst, in_=view)
+            else:
+                nc.vector.tensor_copy(out=dst, in_=view)
 
         w_f32 = w_sb[:].bitcast(F32)
         w_grp = const.tile([P, 8 * CIN], BF16, name="w_grp", align_bytes=64)
         w_grp_f32 = w_grp[:].bitcast(F32)
         w_codes = const.tile([P, E * COUT], U32, name="w_codes", align_bytes=64)
         w_scl = const.tile([P, E * COUT], U8, name="w_scl", align_bytes=64)
+        wts = []
         for q in range(4):
-            wt = ring(psum, ("pa" if q % 2 == 0 else "pb"), q // 2 + 1, 3, [P, 512], F32, 0)
+            wt = bank("pa" if q % 2 == 0 else "pb", q // 2 + 1, 3)
             transposes(wt, w_f32, 2 * q)
-            regroup("s" if q % 2 == 0 else "v", w_grp_f32, q, wt)
-        for h in range(2):
-            nc.vector.quantize_mx(out=w_codes[:, h * 512:(h + 1) * 512].bitcast(FP8X4),
-                                  scales=w_scl[:, h * 512:(h + 1) * 512],
-                                  in_=w_grp[:, h * 2048:(h + 1) * 2048])
+            wts.append(wt)
 
         grp = {}
-        banks = {}
+        xt = {}
         codes = {}
         scl = {}
         u_t = {}
         a1_t = {}
         o_t = {}
         k_t = {}
-        pab = {}
+        pa_t = {}
+        pb_t = {}
         sa0_t = {}
+        acc1_t = {}
+        acc_t = {}
 
-        def stage_t(g):
-            grp[g] = ring(rings, "grp", g, 3, [P, GT * CIN], BF16, 64)
+        def t_pe(g):
             xf = xs[g][:].bitcast(F32)
             for h in range(2):
-                bank = ring(psum, "xt", 2 * g + h, 2, [P, 512], F32, 0)
-                transposes(bank, xf, 2 * h)
-                banks[(g, h)] = bank
+                xt[(g, h)] = bank("xt", 2 * g + h, 2)
+                transposes(xt[(g, h)], xf, 2 * h)
 
-        def stage_exit(g, h):
-            regroup(EXIT_ENG[h], grp[g][:].bitcast(F32), h, banks[(g, h)])
+        def x_out(g, h, eng):
+            if h == 0:
+                grp[g] = ring("grp", g, 3, [P, GT * CIN], BF16)
+            regroup(eng, grp[g][:].bitcast(F32), h, xt[(g, h)])
 
-        def stage_q(g):
-            codes[g] = ring(rings, "codes", g, 3, [P, GT * P], U32, 64)
-            scl[g] = ring(rings, "scl", g, 3, [P, GT * P], U8, 64)
+        def quant(g):
+            codes[g] = ring("codes", g, 3, [P, GT * P], U32)
+            scl[g] = ring("scl", g, 3, [P, GT * P], U8)
             nc.vector.quantize_mx(out=codes[g][:].bitcast(FP8X4), scales=scl[g][:], in_=grp[g][:])
 
         def gcol(j, t):
             return gs[:, j * E + t:j * E + t + 1]
 
-        def is_two(g, jj):
-            return jj >= GT - NTWO[g]
+        def is_two(j):
+            return j % GT >= GT - NTWO[j // GT]
 
-        def stage_mm(g, jj):
-            if jj == 0:
-                u_t[g] = ring(rings, "u", g, 4, [P, GW], F32)
-                k_t[g] = ring(rings, "k", g, 4, [P, GW], I32)
-                o_t[g] = ring(rings, "o", g, 5, [P, GW], F32)
-                if NTWO[g] > 0:
-                    a1_t[g] = ring(rings, "a1", g, 4, [P, 3 * COUT], F32)
-            j = g * GT + jj
-            pa = ring(psum, "pa", j + 3, 3, [P, 512], F32, 0)
-            pb = ring(psum, "pb", j + 3, 3, [P, 512], F32, 0)
-            pab[j] = (pa, pb)
-            for h, bank in ((0, pa), (1, pb)):
-                nc.tensor.matmul_mx(out=bank[:],
-                                    lhsT=codes[g][:, jj * P:(jj + 1) * P].bitcast(FP8X4),
-                                    lhsT_scale=scl[g][:, jj * P:(jj + 1) * P],
-                                    rhs=w_codes[:, h * 512:(h + 1) * 512].bitcast(FP8X4),
-                                    rhs_scale=w_scl[:, h * 512:(h + 1) * 512],
-                                    start=True, stop=True)
-            sa0 = ring(rings, "sa0", j, 6, [P, COUT], F32)
-            sa0_t[j] = sa0
-            nc.scalar.activation(out=sa0[:], in_=pa[:, 0:COUT], func=ACT.Copy, scale=gcol(j, 0))
-            if is_two(g, jj):
-                c = (jj - (GT - NTWO[g])) * COUT
-                nc.scalar.activation(out=a1_t[g][:, c:c + COUT], in_=pa[:, COUT:2 * COUT],
-                                     func=ACT.Copy, scale=gcol(j, 1))
-
-        def stage_stt(g, jj):
-            j = g * GT + jj
-            pa, pb = pab[j]
-
-            def stt(dst, src, t, add):
-                nc.vector.scalar_tensor_tensor(out=dst, in0=src, scalar=gcol(j, t), in1=add,
-                                               op0=ALU.mult, op1=ALU.add)
-
-            acc = ring(rings, "acc", j, 3, [P, COUT], F32)
-            if is_two(g, jj):
-                stt(acc[:], pb[:, 0:COUT], 2, sa0_t[j][:])
+        def mx(j, h):
+            g, jj = j // GT, j % GT
+            dst = bank("pa" if h == 0 else "pb", j + 3, 3)
+            if h == 0:
+                pa_t[j] = dst
             else:
-                acc1 = ring(rings, "acc1", j, 3, [P, COUT], F32)
-                stt(acc1[:], pa[:, COUT:2 * COUT], 1, sa0_t[j][:])
-                stt(acc[:], pb[:, 0:COUT], 2, acc1[:])
-            stt(u_t[g][:, jj * COUT:(jj + 1) * COUT], pb[:, COUT:2 * COUT], 3, acc[:])
+                pb_t[j] = dst
+            nc.tensor.matmul_mx(out=dst[:],
+                                lhsT=codes[g][:, jj * P:(jj + 1) * P].bitcast(FP8X4),
+                                lhsT_scale=scl[g][:, jj * P:(jj + 1) * P],
+                                rhs=w_codes[:, h * 512:(h + 1) * 512].bitcast(FP8X4),
+                                rhs_scale=w_scl[:, h * 512:(h + 1) * 512],
+                                start=True, stop=True)
 
-        def stage_add_cast(g):
+        def p0(j):
+            sa0_t[j] = ring("sa0", j, 8, [P, COUT], F32)
+            nc.scalar.activation(out=sa0_t[j][:], in_=pa_t[j][:, 0:COUT], func=ACT.Copy,
+                                 scale=gcol(j, 0))
+
+        def p1(j):
+            g, jj = j // GT, j % GT
+            if g not in a1_t:
+                a1_t[g] = ring("a1", g, 3, [P, 3 * COUT], F32)
+            c = (jj - (GT - NTWO[g])) * COUT
+            nc.scalar.activation(out=a1_t[g][:, c:c + COUT], in_=pa_t[j][:, COUT:2 * COUT],
+                                 func=ACT.Copy, scale=gcol(j, 1))
+
+        def stt(dst, src, j, t, add):
+            nc.vector.scalar_tensor_tensor(out=dst, in0=src, scalar=gcol(j, t), in1=add,
+                                           op0=ALU.mult, op1=ALU.add)
+
+        def s1(j):
+            acc1_t[j] = ring("acc1", j, 4, [P, COUT], F32)
+            stt(acc1_t[j][:], pa_t[j][:, COUT:2 * COUT], j, 1, sa0_t[j][:])
+
+        def s2(j):
+            acc_t[j] = ring("acc", j, 4, [P, COUT], F32)
+            stt(acc_t[j][:], pb_t[j][:, 0:COUT], j, 2, sa0_t[j][:] if is_two(j) else acc1_t[j][:])
+
+        def s3(j):
+            g, jj = j // GT, j % GT
+            if g not in u_t:
+                u_t[g] = ring("u", g, 5, [P, GW], F32)
+            stt(u_t[g][:, jj * COUT:(jj + 1) * COUT], pb_t[j][:, COUT:2 * COUT], j, 3, acc_t[j][:])
+
+        def chain(j):
+            return [s2, s3] if is_two(j) else [s1, s2, s3]
+
+        def pair(ja, jb, first=0, stop=3):
+            ca, cb = chain(ja), chain(jb)
+            for n in range(first, stop):
+                if n < len(ca):
+                    ca[n](ja)
+                if n < len(cb):
+                    cb[n](jb)
+
+        def add_cast(g):
             if NTWO[g] > 0:
                 lo = (GT - NTWO[g]) * COUT
-                nc.gpsimd.tensor_tensor(out=u_t[g][:, lo:GW], in0=u_t[g][:, lo:GW], in1=a1_t[g][:, 0:NTWO[g] * COUT],
-                                        op=ALU.add)
+                nc.gpsimd.tensor_tensor(out=u_t[g][:, lo:GW], in0=u_t[g][:, lo:GW],
+                                        in1=a1_t[g][:, 0:NTWO[g] * COUT], op=ALU.add)
+            k_t[g] = ring("k", g, 3, [P, GW], I32)
             nc.gpsimd.tensor_scalar(out=k_t[g][:], in0=u_t[g][:], scalar1=1.0, scalar2=0.0,
                                     op0=ALU.mult, op1=ALU.add)
 
         def cast_v(g, lo, hi):
+            if g not in k_t:
+                k_t[g] = ring("k", g, 3, [P, GW], I32)
             nc.vector.tensor_copy(out=k_t[g][:, lo:hi], in_=u_t[g][:, lo:hi])
 
-        def sub(g, lo, hi):
+        def sub(g, lo=0, hi=GW):
             nc.vector.tensor_tensor(out=u_t[g][:, lo:hi], in0=u_t[g][:, lo:hi], in1=k_t[g][:, lo:hi],
                                     op=ALU.subtract)
 
         def sin(g, lo, hi):
+            if g not in o_t:
+                o_t[g] = ring("o", g, 3, [P, GW], F32)
             nc.scalar.activation(out=o_t[g][:, lo:hi], in_=u_t[g][:, lo:hi], func=ACT.Sin,
                                  scale=2.0 * math.pi)
 
-        def store(g, lo, hi):
+        def store(g, lo=0, hi=GW):
             nc.sync.dma_start(out=o_v[:, g * GW + lo:g * GW + hi], in_=o_t[g][:, lo:hi])
 
-        for i in range(-2, NG + 1):
-            tg, qg, mg, ag, rg = i + 2, i + 1, i, i - 1, i - 2
-            has_t = tg < NG
-            has_q = 0 <= qg < NG
-            has_m = 0 <= mg < NG
-            if has_t:
-                stage_t(tg)
-            if 0 <= ag < last:
-                stage_add_cast(ag)
-            for s in range(GT):
-                if has_m:
-                    stage_mm(mg, s)
-                if has_t and s < 2:
-                    stage_exit(tg, s)
-                if 0 <= rg < last - 1 and s >= 2:
-                    sin(rg, (s - 2) * 512, (s - 1) * 512)
-                    if s == 3:
-                        store(rg, 0, GW)
-                if mg == last and s >= 1:
-                    sin(mg, (s - 1) * COUT, s * COUT)
-                    store(mg, (s - 1) * COUT, s * COUT)
-                if mg == last and s == 3:
-                    sin(last - 1, 0, GW)
-                    store(last - 1, 0, GW)
-                if has_m:
-                    stage_stt(mg, s)
-                if 0 <= rg < last - 1 and s == 0:
-                    sub(rg, 0, GW)
-                if has_q and s == 2:
-                    stage_q(qg)
-                if mg == last:
-                    cast_v(mg, s * COUT, (s + 1) * COUT)
-                    sub(mg, s * COUT, (s + 1) * COUT)
-                    if s == 2:
-                        sub(last - 1, 0, GW)
-        sin(last, 3 * COUT, GW)
-        store(last, 3 * COUT, GW)
+        def sin_store(g):
+            sin(g, 0, 512)
+            sin(g, 512, GW)
+            store(g)
+
+        t_pe(0)
+        t_pe(1)
+        for q in range(4):
+            regroup("s" if q % 2 == 0 else "v", w_grp_f32, q, wts[q])
+            if q % 2 == 1:
+                h = q // 2
+                nc.vector.quantize_mx(out=w_codes[:, h * 512:(h + 1) * 512].bitcast(FP8X4),
+                                      scales=w_scl[:, h * 512:(h + 1) * 512],
+                                      in_=w_grp[:, h * 2048:(h + 1) * 2048])
+        x_out(0, 0, "s")
+        x_out(0, 1, "v")
+        quant(0)
+        x_out(1, 0, "s")
+        x_out(1, 1, "s")
+
+        for i in range(0, last):
+            j = i * GT
+            if i + 2 < NG:
+                t_pe(i + 2)
+            if i >= 1:
+                add_cast(i - 1)
+            for ja in (j, j + 2):
+                mx(ja, 0)
+                mx(ja + 1, 0)
+                mx(ja, 1)
+                mx(ja + 1, 1)
+            p0(j)
+            p0(j + 1)
+            if is_two(j + 1):
+                p1(j + 1)
+            if i + 2 < NG:
+                x_out(i + 2, 0, "s")
+            p0(j + 2)
+            p0(j + 3)
+            if is_two(j + 2):
+                p1(j + 2)
+            if is_two(j + 3):
+                p1(j + 3)
+            if i + 2 < NG:
+                x_out(i + 2, 1, "s")
+            if i >= 3:
+                sin_store(i - 3)
+            pair(j, j + 1)
+            quant(i + 1)
+            pair(j + 2, j + 3)
+            if i >= 2:
+                sub(i - 2)
+
+        j = last * GT
+        add_cast(last - 1)
+        for ja in (j, j + 2):
+            mx(ja, 0)
+            mx(ja + 1, 0)
+            mx(ja, 1)
+            mx(ja + 1, 1)
+        for jj in range(GT):
+            p0(j + jj)
+        sin_store(last - 3)
+        pair(j, j + 1)
+        sub(last - 2)
+        cast_v(last, 0, 512)
+        pair(j + 2, j + 3, 0, 1)
+        sub(last, 0, 512)
+        sin_store(last - 2)
+        sin(last, 0, 512)
+        store(last, 0, 512)
+        sub(last - 1)
+        pair(j + 2, j + 3, 1, 3)
+        sin_store(last - 1)
+        cast_v(last, 512, 768)
+        cast_v(last, 768, GW)
+        sub(last, 512, 768)
+        sub(last, 768, GW)
+        sin(last, 512, 768)
+        store(last, 512, 768)
+        sin(last, 768, GW)
+        store(last, 768, GW)

@@ -174,7 +174,7 @@ def tile_sinelayer_loe_pa_t_kernel(tc, in_feats, tile_gate, W, out):
         def s3(j):
             g, jj = j // GT, j % GT
             if g not in u_t:
-                u_t[g] = ring("u", g, 5, [P, GW], F32)
+                u_t[g] = ring("u", g, 4, [P, GW], F32)
             stt(u_t[g][:, jj * COUT:(jj + 1) * COUT], pb_t[j][:, COUT:2 * COUT], j, 3, acc_t[j][:])
 
         def chain(j):
@@ -188,18 +188,21 @@ def tile_sinelayer_loe_pa_t_kernel(tc, in_feats, tile_gate, W, out):
                 if n < len(cb):
                     cb[n](jb)
 
+        def cast_g(g, lo, hi):
+            nc.gpsimd.tensor_scalar(out=k_t[g][:, lo:hi], in0=u_t[g][:, lo:hi], scalar1=1.0,
+                                    scalar2=0.0, op0=ALU.mult, op1=ALU.add)
+
         def add_cast(g):
-            if NTWO[g] > 0:
-                lo = (GT - NTWO[g]) * COUT
-                nc.gpsimd.tensor_tensor(out=u_t[g][:, lo:GW], in0=u_t[g][:, lo:GW],
-                                        in1=a1_t[g][:, 0:NTWO[g] * COUT], op=ALU.add)
-            k_t[g] = ring("k", g, 3, [P, GW], I32)
-            nc.gpsimd.tensor_scalar(out=k_t[g][:], in0=u_t[g][:], scalar1=1.0, scalar2=0.0,
-                                    op0=ALU.mult, op1=ALU.add)
+            k_t[g] = ring("k", g, 1, [P, GW], I32)
+            lo = (GT - NTWO[g]) * COUT
+            cast_g(g, 0, lo)
+            nc.gpsimd.tensor_tensor(out=u_t[g][:, lo:GW], in0=u_t[g][:, lo:GW],
+                                    in1=a1_t[g][:, 0:NTWO[g] * COUT], op=ALU.add)
+            cast_g(g, lo, GW)
 
         def cast_v(g, lo, hi):
             if g not in k_t:
-                k_t[g] = ring("k", g, 3, [P, GW], I32)
+                k_t[g] = ring("k", g, 1, [P, GW], I32)
             nc.vector.tensor_copy(out=k_t[g][:, lo:hi], in_=u_t[g][:, lo:hi])
 
         def sub(g, lo=0, hi=GW):
@@ -260,13 +263,13 @@ def tile_sinelayer_loe_pa_t_kernel(tc, in_feats, tile_gate, W, out):
                 p1(j + 3)
             if i + 2 < NG:
                 x_out(i + 2, 1, "s")
-            if i >= 3:
-                sin_store(i - 3)
-            pair(j, j + 1)
-            quant(i + 1)
-            pair(j + 2, j + 3)
             if i >= 2:
-                sub(i - 2)
+                sin_store(i - 2)
+            pair(j, j + 1)
+            pair(j + 2, j + 3)
+            quant(i + 1)
+            if i >= 1:
+                sub(i - 1)
 
         j = last * GT
         add_cast(last - 1)
@@ -277,23 +280,16 @@ def tile_sinelayer_loe_pa_t_kernel(tc, in_feats, tile_gate, W, out):
             mx(ja + 1, 1)
         for jj in range(GT):
             p0(j + jj)
-        sin_store(last - 3)
-        pair(j, j + 1)
-        sub(last - 2)
-        cast_v(last, 0, 512)
-        pair(j + 2, j + 3, 0, 1)
-        sub(last, 0, 512)
         sin_store(last - 2)
-        sin(last, 0, 512)
-        store(last, 0, 512)
+        pair(j, j + 1)
+        pair(j + 2, j + 3)
         sub(last - 1)
-        pair(j + 2, j + 3, 1, 3)
         sin_store(last - 1)
-        cast_v(last, 512, 768)
-        cast_v(last, 768, GW)
+        cast_v(last, 0, 512)
+        cast_v(last, 512, GW)
+        sub(last, 0, 512)
         sub(last, 512, 768)
         sub(last, 768, GW)
-        sin(last, 512, 768)
-        store(last, 512, 768)
-        sin(last, 768, GW)
-        store(last, 768, GW)
+        for lo, hi in ((0, 512), (512, 768), (768, GW)):
+            sin(last, lo, hi)
+            store(last, lo, hi)

@@ -18,11 +18,13 @@ B, CIN, COUT, E = 8192, 512, 256, 4
 NT = B // P
 GT = 4
 NG = NT // GT
-GW = GT * COUT
 FLOPS = 2 * B * CIN * COUT * E
 
-MANUAL = True
-NTWO = (2,) * 15 + (0,)
+MANUAL = False
+TWO = (False, True, False, True)
+EXIT_ENG = ("s", "s")
+CAST_ENG = ("s", "g")
+MAGIC = 12582912.0
 
 
 def tile_sinelayer_loe_pa_t_kernel(tc, in_feats, tile_gate, W, out):
@@ -31,22 +33,16 @@ def tile_sinelayer_loe_pa_t_kernel(tc, in_feats, tile_gate, W, out):
     g_v = tile_gate.rearrange("(p r) e -> p (r e)", p=P)
     w_v = W.rearrange("t (h p) k -> p (t h) k", p=P)
     o_v = out.rearrange("(p r) c -> p (r c)", p=P)
-    last = NG - 1
 
     with ExitStack() as ctx:
         if MANUAL:
             ctx.enter_context(tc.manual_schedule())
         const = ctx.enter_context(tc.tile_pool(name="const", bufs=1))
-        rings = ctx.enter_context(tc.tile_pool(name="rings", bufs=1))
-        psum = ctx.enter_context(tc.psum_pool(name="psum", bufs=1))
-
-        def ring(base, idx, depth, shape, dtype):
-            return rings.tile(shape, dtype, tag="%s_s%d" % (base, idx % depth),
-                              name="%s_%d" % (base, idx), align_bytes=64)
-
-        def bank(base, idx, depth):
-            return psum.tile([P, 512], F32, tag="%s_s%d" % (base, idx % depth),
-                             name="%s_%d" % (base, idx))
+        gpool = ctx.enter_context(tc.tile_pool(name="gpool", bufs=3))
+        spool = ctx.enter_context(tc.tile_pool(name="spool", bufs=4))
+        rpool = ctx.enter_context(tc.tile_pool(name="rpool", bufs=3))
+        psx = ctx.enter_context(tc.psum_pool(name="psx", bufs=2))
+        psp = ctx.enter_context(tc.psum_pool(name="psp", bufs=3))
 
         w_sb = const.tile([P, 8 * CIN], BF16, name="w_sb")
         w_sb3 = w_sb[:].rearrange("p (a k) -> p a k", a=8)
@@ -70,226 +66,149 @@ def tile_sinelayer_loe_pa_t_kernel(tc, in_feats, tile_gate, W, out):
         nc.vector.tensor_scalar(out=gs[:], in0=gate_sb[:], scalar1=30.0 / (2.0 * math.pi),
                                 scalar2=None, op0=ALU.mult)
 
-        def transposes(dst, src_f32, first):
+        def copy_out(eng, dst, src):
+            if eng == "s":
+                nc.scalar.copy(out=dst, in_=src)
+            else:
+                nc.vector.tensor_copy(out=dst, in_=src)
+
+        def transposes(bank, src_f32, first):
             for jj in range(2):
                 for u in range(2):
                     c = (first + jj) * 256 + u * P
-                    nc.tensor.transpose(dst[:, (jj * 2 + u) * P:(jj * 2 + u + 1) * P],
+                    nc.tensor.transpose(bank[:, (jj * 2 + u) * P:(jj * 2 + u + 1) * P],
                                         src_f32[:, c:c + P], ident[:])
 
-        def regroup(eng, grp_f32, h, src):
-            dst = grp_f32[:, h * 512:(h + 1) * 512].rearrange("p (j m u) -> p j m u", j=2, u=2)
-            view = src[:].rearrange("p (j u m) -> p j m u", j=2, u=2)
-            if eng == "s":
-                nc.scalar.copy(out=dst, in_=view)
-            else:
-                nc.vector.tensor_copy(out=dst, in_=view)
+        def regroup(eng, grp_f32, h, bank):
+            copy_out(eng,
+                     grp_f32[:, h * 512:(h + 1) * 512].rearrange("p (j m u) -> p j m u", j=2, u=2),
+                     bank[:].rearrange("p (j u m) -> p j m u", j=2, u=2))
 
         w_f32 = w_sb[:].bitcast(F32)
         w_grp = const.tile([P, 8 * CIN], BF16, name="w_grp", align_bytes=64)
         w_grp_f32 = w_grp[:].bitcast(F32)
         w_codes = const.tile([P, E * COUT], U32, name="w_codes", align_bytes=64)
         w_scl = const.tile([P, E * COUT], U8, name="w_scl", align_bytes=64)
-        wts = []
         for q in range(4):
-            wt = bank("pa" if q % 2 == 0 else "pb", q // 2 + 1, 3)
+            wt = psp.tile([P, 512], F32, tag=("pa" if q % 2 == 0 else "pb"), name="wt%d" % q)
             transposes(wt, w_f32, 2 * q)
-            wts.append(wt)
+            regroup("s" if q % 2 == 0 else "v", w_grp_f32, q, wt)
+        for h in range(2):
+            nc.vector.quantize_mx(out=w_codes[:, h * 512:(h + 1) * 512].bitcast(FP8X4),
+                                  scales=w_scl[:, h * 512:(h + 1) * 512],
+                                  in_=w_grp[:, h * 2048:(h + 1) * 2048])
 
         grp = {}
-        xt = {}
+        banks = {}
         codes = {}
         scl = {}
         u_t = {}
-        a1_t = {}
         o_t = {}
         k_t = {}
-        pa_t = {}
-        pb_t = {}
-        sa0_t = {}
-        acc1_t = {}
-        acc_t = {}
+        r_t = {}
 
-        def t_pe(g):
+        def stage_t(g):
+            grp[g] = gpool.tile([P, GT * CIN], BF16, tag="grp", name="grp%d" % g, align_bytes=64)
             xf = xs[g][:].bitcast(F32)
             for h in range(2):
-                xt[(g, h)] = bank("xt", 2 * g + h, 2)
-                transposes(xt[(g, h)], xf, 2 * h)
+                bank = psx.tile([P, 512], F32, tag="xt", name="xt%d_%d" % (g, h))
+                transposes(bank, xf, 2 * h)
+                banks[(g, h)] = bank
 
-        def x_out(g, h, eng):
-            if h == 0:
-                grp[g] = ring("grp", g, 3, [P, GT * CIN], BF16)
-            regroup(eng, grp[g][:].bitcast(F32), h, xt[(g, h)])
+        def stage_exit(g, h):
+            regroup(EXIT_ENG[h], grp[g][:].bitcast(F32), h, banks[(g, h)])
 
-        def quant(g):
-            codes[g] = ring("codes", g, 3, [P, GT * P], U32)
-            scl[g] = ring("scl", g, 3, [P, GT * P], U8)
+        def stage_q(g):
+            codes[g] = gpool.tile([P, GT * P], U32, tag="codes", name="codes%d" % g, align_bytes=64)
+            scl[g] = gpool.tile([P, GT * P], U8, tag="scl", name="scl%d" % g, align_bytes=64)
             nc.vector.quantize_mx(out=codes[g][:].bitcast(FP8X4), scales=scl[g][:], in_=grp[g][:])
 
-        def gcol(j, t):
-            return gs[:, j * E + t:j * E + t + 1]
+        def stage_m(g, jj):
+            if jj == 0:
+                u_t[g] = rpool.tile([P, GT * COUT], F32, tag="u", name="u%d" % g)
+            j = g * GT + jj
+            pa = psp.tile([P, 512], F32, tag="pa", name="pa%d" % j)
+            pb = psp.tile([P, 512], F32, tag="pb", name="pb%d" % j)
+            for h, bank in ((0, pa), (1, pb)):
+                nc.tensor.matmul_mx(out=bank[:],
+                                    lhsT=codes[g][:, jj * P:(jj + 1) * P].bitcast(FP8X4),
+                                    lhsT_scale=scl[g][:, jj * P:(jj + 1) * P],
+                                    rhs=w_codes[:, h * 512:(h + 1) * 512].bitcast(FP8X4),
+                                    rhs_scale=w_scl[:, h * 512:(h + 1) * 512],
+                                    start=True, stop=True)
 
-        def is_two(j):
-            return j % GT >= GT - NTWO[j // GT]
+            def gcol(t):
+                return gs[:, j * E + t:j * E + t + 1]
 
-        def mx(j, h):
-            g, jj = j // GT, j % GT
-            dst = bank("pa" if h == 0 else "pb", j + 3, 3)
-            if h == 0:
-                pa_t[j] = dst
+            def stt(dst, src, t, add):
+                nc.vector.scalar_tensor_tensor(out=dst, in0=src, scalar=gcol(t), in1=add,
+                                               op0=ALU.mult, op1=ALU.add)
+
+            u_dst = u_t[g][:, jj * COUT:(jj + 1) * COUT]
+            sa0 = spool.tile([P, COUT], F32, tag="sa0", name="sa0_%d" % j)
+            nc.scalar.activation(out=sa0[:], in_=pa[:, 0:COUT], func=ACT.Copy, scale=gcol(0))
+            acc = spool.tile([P, COUT], F32, tag="acc", name="acc%d" % j)
+            if TWO[jj]:
+                sa1 = spool.tile([P, COUT], F32, tag="sa1", name="sa1_%d" % j)
+                nc.scalar.activation(out=sa1[:], in_=pa[:, COUT:2 * COUT], func=ACT.Copy, scale=gcol(1))
+                a01 = spool.tile([P, COUT], F32, tag="a01", name="a01_%d" % j)
+                nc.gpsimd.tensor_tensor(out=a01[:], in0=sa0[:], in1=sa1[:], op=ALU.add)
+                stt(acc[:], pb[:, 0:COUT], 2, a01[:])
             else:
-                pb_t[j] = dst
-            nc.tensor.matmul_mx(out=dst[:],
-                                lhsT=codes[g][:, jj * P:(jj + 1) * P].bitcast(FP8X4),
-                                lhsT_scale=scl[g][:, jj * P:(jj + 1) * P],
-                                rhs=w_codes[:, h * 512:(h + 1) * 512].bitcast(FP8X4),
-                                rhs_scale=w_scl[:, h * 512:(h + 1) * 512],
-                                start=True, stop=True)
+                acc1 = spool.tile([P, COUT], F32, tag="acc1", name="acc1_%d" % j)
+                stt(acc1[:], pa[:, COUT:2 * COUT], 1, sa0[:])
+                stt(acc[:], pb[:, 0:COUT], 2, acc1[:])
+            stt(u_dst, pb[:, COUT:2 * COUT], 3, acc[:])
 
-        def p0(j):
-            sa0_t[j] = ring("sa0", j, 8, [P, COUT], F32)
-            nc.scalar.activation(out=sa0_t[j][:], in_=pa_t[j][:, 0:COUT], func=ACT.Copy,
-                                 scale=gcol(j, 0))
+        def stage_cast(g, h):
+            k_t[(g, h)] = rpool.tile([P, 512], I32, tag="k", name="k%d_%d" % (g, h))
+            src = u_t[g][:, h * 512:(h + 1) * 512]
+            if CAST_ENG[h] == "g":
+                nc.gpsimd.tensor_scalar(out=k_t[(g, h)][:], in0=src, scalar1=1.0, scalar2=0.0,
+                                        op0=ALU.mult, op1=ALU.add)
+            else:
+                nc.scalar.activation(out=k_t[(g, h)][:].bitcast(U32), in_=src, func=ACT.Copy,
+                                     bias=MAGIC, scale=1.0)
 
-        def p1(j):
-            g, jj = j // GT, j % GT
-            if g not in a1_t:
-                a1_t[g] = ring("a1", g, 3, [P, 3 * COUT], F32)
-            c = (jj - (GT - NTWO[g])) * COUT
-            nc.scalar.activation(out=a1_t[g][:, c:c + COUT], in_=pa_t[j][:, COUT:2 * COUT],
-                                 func=ACT.Copy, scale=gcol(j, 1))
+        def stage_sub(g, h):
+            r_t[(g, h)] = rpool.tile([P, 512], F32, tag="r", name="r%d_%d" % (g, h))
+            src = u_t[g][:, h * 512:(h + 1) * 512]
+            if CAST_ENG[h] == "g":
+                nc.vector.tensor_tensor(out=r_t[(g, h)][:], in0=k_t[(g, h)][:], in1=src, op=ALU.subtract)
+            else:
+                nc.vector.scalar_tensor_tensor(out=r_t[(g, h)][:], in0=k_t[(g, h)][:], scalar=MAGIC,
+                                               in1=src, op0=ALU.subtract, op1=ALU.subtract)
 
-        def stt(dst, src, j, t, add):
-            nc.vector.scalar_tensor_tensor(out=dst, in0=src, scalar=gcol(j, t), in1=add,
-                                           op0=ALU.mult, op1=ALU.add)
+        def stage_sin(g, h):
+            if h == 0:
+                o_t[g] = rpool.tile([P, GT * COUT], F32, tag="o", name="o%d" % g)
+            nc.scalar.activation(out=o_t[g][:, h * 512:(h + 1) * 512], in_=r_t[(g, h)][:],
+                                 func=ACT.Sin, scale=-2.0 * math.pi)
+            if h == 1:
+                nc.sync.dma_start(out=o_v[:, g * GT * COUT:(g + 1) * GT * COUT], in_=o_t[g][:])
 
-        def s1(j):
-            acc1_t[j] = ring("acc1", j, 4, [P, COUT], F32)
-            stt(acc1_t[j][:], pa_t[j][:, COUT:2 * COUT], j, 1, sa0_t[j][:])
-
-        def s2(j):
-            acc_t[j] = ring("acc", j, 4, [P, COUT], F32)
-            stt(acc_t[j][:], pb_t[j][:, 0:COUT], j, 2, sa0_t[j][:] if is_two(j) else acc1_t[j][:])
-
-        def s3(j):
-            g, jj = j // GT, j % GT
-            if g not in u_t:
-                u_t[g] = ring("u", g, 4, [P, GW], F32)
-            stt(u_t[g][:, jj * COUT:(jj + 1) * COUT], pb_t[j][:, COUT:2 * COUT], j, 3, acc_t[j][:])
-
-        def chain(j):
-            return [s2, s3] if is_two(j) else [s1, s2, s3]
-
-        def pair(ja, jb, first=0, stop=3):
-            ca, cb = chain(ja), chain(jb)
-            for n in range(first, stop):
-                if n < len(ca):
-                    ca[n](ja)
-                if n < len(cb):
-                    cb[n](jb)
-
-        def cast_g(g, lo, hi):
-            nc.gpsimd.tensor_scalar(out=k_t[g][:, lo:hi], in0=u_t[g][:, lo:hi], scalar1=1.0,
-                                    scalar2=0.0, op0=ALU.mult, op1=ALU.add)
-
-        def add_cast(g):
-            k_t[g] = ring("k", g, 1, [P, GW], I32)
-            lo = (GT - NTWO[g]) * COUT
-            cast_g(g, 0, lo)
-            nc.gpsimd.tensor_tensor(out=u_t[g][:, lo:GW], in0=u_t[g][:, lo:GW],
-                                    in1=a1_t[g][:, 0:NTWO[g] * COUT], op=ALU.add)
-            cast_g(g, lo, GW)
-
-        def cast_v(g, lo, hi):
-            if g not in k_t:
-                k_t[g] = ring("k", g, 1, [P, GW], I32)
-            nc.vector.tensor_copy(out=k_t[g][:, lo:hi], in_=u_t[g][:, lo:hi])
-
-        def sub(g, lo=0, hi=GW):
-            nc.vector.tensor_tensor(out=u_t[g][:, lo:hi], in0=u_t[g][:, lo:hi], in1=k_t[g][:, lo:hi],
-                                    op=ALU.subtract)
-
-        def sin(g, lo, hi):
-            if g not in o_t:
-                o_t[g] = ring("o", g, 3, [P, GW], F32)
-            nc.scalar.activation(out=o_t[g][:, lo:hi], in_=u_t[g][:, lo:hi], func=ACT.Sin,
-                                 scale=2.0 * math.pi)
-
-        def store(g, lo=0, hi=GW):
-            nc.sync.dma_start(out=o_v[:, g * GW + lo:g * GW + hi], in_=o_t[g][:, lo:hi])
-
-        def sin_store(g):
-            sin(g, 0, 512)
-            sin(g, 512, GW)
-            store(g)
-
-        t_pe(0)
-        t_pe(1)
-        for q in range(4):
-            regroup("s" if q % 2 == 0 else "v", w_grp_f32, q, wts[q])
-            if q % 2 == 1:
-                h = q // 2
-                nc.vector.quantize_mx(out=w_codes[:, h * 512:(h + 1) * 512].bitcast(FP8X4),
-                                      scales=w_scl[:, h * 512:(h + 1) * 512],
-                                      in_=w_grp[:, h * 2048:(h + 1) * 2048])
-        x_out(0, 0, "s")
-        x_out(0, 1, "v")
-        quant(0)
-        x_out(1, 0, "s")
-        x_out(1, 1, "s")
-
-        for i in range(0, last):
-            j = i * GT
-            if i + 2 < NG:
-                t_pe(i + 2)
-            if i >= 1:
-                add_cast(i - 1)
-            for ja in (j, j + 2):
-                mx(ja, 0)
-                mx(ja + 1, 0)
-                mx(ja, 1)
-                mx(ja + 1, 1)
-            p0(j)
-            p0(j + 1)
-            if is_two(j + 1):
-                p1(j + 1)
-            if i + 2 < NG:
-                x_out(i + 2, 0, "s")
-            p0(j + 2)
-            p0(j + 3)
-            if is_two(j + 2):
-                p1(j + 2)
-            if is_two(j + 3):
-                p1(j + 3)
-            if i + 2 < NG:
-                x_out(i + 2, 1, "s")
-            if i >= 2:
-                sin_store(i - 2)
-            pair(j, j + 1)
-            pair(j + 2, j + 3)
-            quant(i + 1)
-            if i >= 1:
-                sub(i - 1)
-
-        j = last * GT
-        add_cast(last - 1)
-        for ja in (j, j + 2):
-            mx(ja, 0)
-            mx(ja + 1, 0)
-            mx(ja, 1)
-            mx(ja + 1, 1)
-        for jj in range(GT):
-            p0(j + jj)
-        sin_store(last - 2)
-        pair(j, j + 1)
-        pair(j + 2, j + 3)
-        sub(last - 1)
-        sin_store(last - 1)
-        cast_v(last, 0, 512)
-        cast_v(last, 512, GW)
-        sub(last, 0, 512)
-        sub(last, 512, 768)
-        sub(last, 768, GW)
-        for lo, hi in ((0, 512), (512, 768), (768, GW)):
-            sin(last, lo, hi)
-            store(last, lo, hi)
+        for i in range(-2, NG + 1):
+            tg, qg, mg, rg = i + 2, i + 1, i, i - 1
+            has_t = tg < NG
+            has_q = 0 <= qg < NG
+            has_m = 0 <= mg < NG
+            has_r = 0 <= rg
+            if has_t:
+                stage_t(tg)
+            for s in range(GT):
+                if has_r and s == 0:
+                    stage_cast(rg, 0)
+                if has_m:
+                    stage_m(mg, s)
+                if has_r and s == 1:
+                    stage_cast(rg, 1)
+                if has_r and s == 0:
+                    stage_sub(rg, 0)
+                if has_q and s == 1:
+                    stage_q(qg)
+                if has_r and s == 2:
+                    stage_sub(rg, 1)
+                if has_t and s < 2:
+                    stage_exit(tg, s)
+                if has_r and s >= 2:
+                    stage_sin(rg, s - 2)

@@ -21,10 +21,11 @@ NG = NT // GT
 FLOPS = 2 * B * CIN * COUT * E
 
 MANUAL = False
-TWO = (False, True, False, True)
+TWO = (False, False, False, True)
 EXIT_ENG = ("s", "s")
-CAST_ENG = ("s", "g")
-MAGIC = 12582912.0
+CAST_ENG = "g"
+LEAD_T = 2
+LEAD_Q = 1
 
 
 def tile_sinelayer_loe_pa_t_kernel(tc, in_feats, tile_gate, W, out):
@@ -38,7 +39,7 @@ def tile_sinelayer_loe_pa_t_kernel(tc, in_feats, tile_gate, W, out):
         if MANUAL:
             ctx.enter_context(tc.manual_schedule())
         const = ctx.enter_context(tc.tile_pool(name="const", bufs=1))
-        gpool = ctx.enter_context(tc.tile_pool(name="gpool", bufs=3))
+        gpool = ctx.enter_context(tc.tile_pool(name="gpool", bufs=LEAD_T + 2))
         spool = ctx.enter_context(tc.tile_pool(name="spool", bufs=4))
         rpool = ctx.enter_context(tc.tile_pool(name="rpool", bufs=3))
         psx = ctx.enter_context(tc.psum_pool(name="psx", bufs=2))
@@ -46,15 +47,24 @@ def tile_sinelayer_loe_pa_t_kernel(tc, in_feats, tile_gate, W, out):
 
         w_sb = const.tile([P, 8 * CIN], BF16, name="w_sb")
         w_sb3 = w_sb[:].rearrange("p (a k) -> p a k", a=8)
-        for q in range(4):
+        def load_w(q):
             nc.sync.dma_start(out=w_sb3[:, 2 * q:2 * q + 2, :], in_=w_v[:, 2 * q:2 * q + 2, :])
+
         gate_sb = const.tile([P, NT * E], BF16, name="gate_sb")
         nc.scalar.dma_start(out=gate_sb[:], in_=g_v)
         xs = []
         for g in range(NG):
             x_t = const.tile([P, GT * CIN], BF16, name="x%d" % g)
-            nc.sync.dma_start(out=x_t[:], in_=x_v[:, g * GT * CIN:(g + 1) * GT * CIN])
             xs.append(x_t)
+        half = GT * CIN // 2
+        load_w(0)
+        load_w(1)
+        nc.sync.dma_start(out=xs[0][:, 0:half], in_=x_v[:, 0:half])
+        load_w(2)
+        load_w(3)
+        nc.sync.dma_start(out=xs[0][:, half:2 * half], in_=x_v[:, half:2 * half])
+        for g in range(1, NG):
+            nc.sync.dma_start(out=xs[g][:], in_=x_v[:, g * GT * CIN:(g + 1) * GT * CIN])
 
         ident = const.tile([P, P], F32, name="ident")
         make_identity(nc, ident[:])
@@ -93,10 +103,11 @@ def tile_sinelayer_loe_pa_t_kernel(tc, in_feats, tile_gate, W, out):
             wt = psp.tile([P, 512], F32, tag=("pa" if q % 2 == 0 else "pb"), name="wt%d" % q)
             transposes(wt, w_f32, 2 * q)
             regroup("s" if q % 2 == 0 else "v", w_grp_f32, q, wt)
-        for h in range(2):
-            nc.vector.quantize_mx(out=w_codes[:, h * 512:(h + 1) * 512].bitcast(FP8X4),
-                                  scales=w_scl[:, h * 512:(h + 1) * 512],
-                                  in_=w_grp[:, h * 2048:(h + 1) * 2048])
+            if q % 2 == 1:
+                h = q // 2
+                nc.vector.quantize_mx(out=w_codes[:, h * 512:(h + 1) * 512].bitcast(FP8X4),
+                                      scales=w_scl[:, h * 512:(h + 1) * 512],
+                                      in_=w_grp[:, h * 2048:(h + 1) * 2048])
 
         grp = {}
         banks = {}
@@ -121,7 +132,11 @@ def tile_sinelayer_loe_pa_t_kernel(tc, in_feats, tile_gate, W, out):
         def stage_q(g):
             codes[g] = gpool.tile([P, GT * P], U32, tag="codes", name="codes%d" % g, align_bytes=64)
             scl[g] = gpool.tile([P, GT * P], U8, tag="scl", name="scl%d" % g, align_bytes=64)
-            nc.vector.quantize_mx(out=codes[g][:].bitcast(FP8X4), scales=scl[g][:], in_=grp[g][:])
+            cuts = ((0, 2), (2, 4)) if g == 0 else ((0, 4),)
+            for lo, hi in cuts:
+                nc.vector.quantize_mx(out=codes[g][:, lo * P:hi * P].bitcast(FP8X4),
+                                      scales=scl[g][:, lo * P:hi * P],
+                                      in_=grp[g][:, lo * CIN:hi * CIN])
 
         def stage_m(g, jj):
             if jj == 0:
@@ -163,36 +178,40 @@ def tile_sinelayer_loe_pa_t_kernel(tc, in_feats, tile_gate, W, out):
         def stage_cast(g, h):
             k_t[(g, h)] = rpool.tile([P, 512], I32, tag="k", name="k%d_%d" % (g, h))
             src = u_t[g][:, h * 512:(h + 1) * 512]
-            if CAST_ENG[h] == "g":
+            if CAST_ENG == "g":
                 nc.gpsimd.tensor_scalar(out=k_t[(g, h)][:], in0=src, scalar1=1.0, scalar2=0.0,
                                         op0=ALU.mult, op1=ALU.add)
             else:
-                nc.scalar.activation(out=k_t[(g, h)][:].bitcast(U32), in_=src, func=ACT.Copy,
-                                     bias=MAGIC, scale=1.0)
+                nc.vector.tensor_copy(out=k_t[(g, h)][:], in_=src)
 
         def stage_sub(g, h):
             r_t[(g, h)] = rpool.tile([P, 512], F32, tag="r", name="r%d_%d" % (g, h))
-            src = u_t[g][:, h * 512:(h + 1) * 512]
-            if CAST_ENG[h] == "g":
-                nc.vector.tensor_tensor(out=r_t[(g, h)][:], in0=k_t[(g, h)][:], in1=src, op=ALU.subtract)
-            else:
-                nc.vector.scalar_tensor_tensor(out=r_t[(g, h)][:], in0=k_t[(g, h)][:], scalar=MAGIC,
-                                               in1=src, op0=ALU.subtract, op1=ALU.subtract)
+            nc.vector.tensor_tensor(out=r_t[(g, h)][:], in0=u_t[g][:, h * 512:(h + 1) * 512],
+                                    in1=k_t[(g, h)][:], op=ALU.subtract)
 
         def stage_sin(g, h):
             if h == 0:
                 o_t[g] = rpool.tile([P, GT * COUT], F32, tag="o", name="o%d" % g)
             nc.scalar.activation(out=o_t[g][:, h * 512:(h + 1) * 512], in_=r_t[(g, h)][:],
-                                 func=ACT.Sin, scale=-2.0 * math.pi)
+                                 func=ACT.Sin, scale=2.0 * math.pi)
             if h == 1:
                 nc.sync.dma_start(out=o_v[:, g * GT * COUT:(g + 1) * GT * COUT], in_=o_t[g][:])
 
-        for i in range(-2, NG + 1):
-            tg, qg, mg, rg = i + 2, i + 1, i, i - 1
+        def tail_piece(g, lo, hi):
+            kk = rpool.tile([P, 256], I32, tag="kk", name="kk%d" % lo)
+            rr = rpool.tile([P, 256], F32, tag="rr", name="rr%d" % lo)
+            oo = rpool.tile([P, 256], F32, tag="oo", name="oo%d" % lo)
+            nc.vector.tensor_copy(out=kk[:], in_=u_t[g][:, lo:hi])
+            nc.vector.tensor_tensor(out=rr[:], in0=u_t[g][:, lo:hi], in1=kk[:], op=ALU.subtract)
+            nc.scalar.activation(out=oo[:], in_=rr[:], func=ACT.Sin, scale=2.0 * math.pi)
+            nc.sync.dma_start(out=o_v[:, g * GT * COUT + lo:g * GT * COUT + hi], in_=oo[:])
+
+        for i in range(-LEAD_T, NG + 1):
+            tg, qg, mg, rg = i + LEAD_T, i + LEAD_Q, i, i - 1
             has_t = tg < NG
             has_q = 0 <= qg < NG
             has_m = 0 <= mg < NG
-            has_r = 0 <= rg
+            has_r = 0 <= rg < NG - 1
             if has_t:
                 stage_t(tg)
             for s in range(GT):
@@ -200,6 +219,8 @@ def tile_sinelayer_loe_pa_t_kernel(tc, in_feats, tile_gate, W, out):
                     stage_cast(rg, 0)
                 if has_m:
                     stage_m(mg, s)
+                    if mg == NG - 1:
+                        tail_piece(mg, s * COUT, (s + 1) * COUT)
                 if has_r and s == 1:
                     stage_cast(rg, 1)
                 if has_r and s == 0:

@@ -21,7 +21,7 @@ NG = NT // GT
 FLOPS = 2 * B * CIN * COUT * E
 
 MANUAL = False
-TWO = (False, False, False, True)
+TWO = (False, True, False, True)
 EXIT_ENG = ("s", "s")
 CAST_ENG = "g"
 LEAD_T = 2

@@ -24,6 +24,7 @@ MANUAL = False
 TWO = (False, True, False, True)
 EXIT_ENG = ("s", "s")
 CAST_ENG = "g"
+WIDE_UNTIL = NG - 2
 LEAD_T = 2
 LEAD_Q = 1
 
@@ -175,9 +176,13 @@ def tile_sinelayer_loe_pa_t_kernel(tc, in_feats, tile_gate, W, out):
                 stt(acc[:], pb[:, 0:COUT], 2, acc1[:])
             stt(u_dst, pb[:, COUT:2 * COUT], 3, acc[:])
 
+        def width(g):
+            return GT * COUT if g < WIDE_UNTIL else GT * COUT // 2
+
         def stage_cast(g, h):
-            k_t[(g, h)] = rpool.tile([P, 512], I32, tag="k", name="k%d_%d" % (g, h))
-            src = u_t[g][:, h * 512:(h + 1) * 512]
+            rw = width(g)
+            k_t[(g, h)] = rpool.tile([P, rw], I32, tag="k", name="k%d_%d" % (g, h))
+            src = u_t[g][:, h * rw:(h + 1) * rw]
             if CAST_ENG == "g":
                 nc.gpsimd.tensor_scalar(out=k_t[(g, h)][:], in0=src, scalar1=1.0, scalar2=0.0,
                                         op0=ALU.mult, op1=ALU.add)
@@ -185,16 +190,18 @@ def tile_sinelayer_loe_pa_t_kernel(tc, in_feats, tile_gate, W, out):
                 nc.vector.tensor_copy(out=k_t[(g, h)][:], in_=src)
 
         def stage_sub(g, h):
-            r_t[(g, h)] = rpool.tile([P, 512], F32, tag="r", name="r%d_%d" % (g, h))
-            nc.vector.tensor_tensor(out=r_t[(g, h)][:], in0=u_t[g][:, h * 512:(h + 1) * 512],
+            rw = width(g)
+            r_t[(g, h)] = rpool.tile([P, rw], F32, tag="r", name="r%d_%d" % (g, h))
+            nc.vector.tensor_tensor(out=r_t[(g, h)][:], in0=u_t[g][:, h * rw:(h + 1) * rw],
                                     in1=k_t[(g, h)][:], op=ALU.subtract)
 
         def stage_sin(g, h):
             if h == 0:
                 o_t[g] = rpool.tile([P, GT * COUT], F32, tag="o", name="o%d" % g)
-            nc.scalar.activation(out=o_t[g][:, h * 512:(h + 1) * 512], in_=r_t[(g, h)][:],
+            rw = width(g)
+            nc.scalar.activation(out=o_t[g][:, h * rw:(h + 1) * rw], in_=r_t[(g, h)][:],
                                  func=ACT.Sin, scale=2.0 * math.pi)
-            if h == 1:
+            if (h + 1) * rw == GT * COUT:
                 nc.sync.dma_start(out=o_v[:, g * GT * COUT:(g + 1) * GT * COUT], in_=o_t[g][:])
 
         def tail_piece(g, lo, hi):
@@ -221,15 +228,18 @@ def tile_sinelayer_loe_pa_t_kernel(tc, in_feats, tile_gate, W, out):
                     stage_m(mg, s)
                     if mg == NG - 1:
                         tail_piece(mg, s * COUT, (s + 1) * COUT)
-                if has_r and s == 1:
+                two_pieces = has_r and rg >= WIDE_UNTIL
+                if two_pieces and s == 1:
                     stage_cast(rg, 1)
-                if has_r and s == 0:
+                if two_pieces and s == 0:
                     stage_sub(rg, 0)
                 if has_q and s == 1:
                     stage_q(qg)
                 if has_r and s == 2:
-                    stage_sub(rg, 1)
+                    stage_sub(rg, 1 if two_pieces else 0)
                 if has_t and s < 2:
                     stage_exit(tg, s)
-                if has_r and s >= 2:
-                    stage_sin(rg, s - 2)
+                if two_pieces and s == 2:
+                    stage_sin(rg, 0)
+                if has_r and s == 3:
+                    stage_sin(rg, 1 if two_pieces else 0)

import math
from contextlib import ExitStack

import concourse.mybir as mybir
from concourse.masks import make_identity

F32 = mybir.dt.float32
BF16 = mybir.dt.bfloat16
I32 = mybir.dt.int32
U32 = mybir.dt.uint32
U8 = mybir.dt.uint8
FP8X4 = mybir.dt.float8_e4m3fn_x4
ALU = mybir.AluOpType
ACT = mybir.ActivationFunctionType

P = 128
B, CIN, COUT, E = 8192, 512, 256, 4
NT = B // P
GT = 4
NG = NT // GT
FLOPS = 2 * B * CIN * COUT * E

MANUAL = False
TWO = (False, True, False, True)
EXIT_ENG = ("s", "s")
CAST_ENG = "g"
WIDE_UNTIL = NG - 2
LEAD_T = 2
LEAD_Q = 1


def tile_sinelayer_loe_pa_t_kernel(tc, in_feats, tile_gate, W, out):
    nc = tc.nc
    x_v = in_feats.rearrange("(p r) k -> p (r k)", p=P)
    g_v = tile_gate.rearrange("(p r) e -> p (r e)", p=P)
    w_v = W.rearrange("t (h p) k -> p (t h) k", p=P)
    o_v = out.rearrange("(p r) c -> p (r c)", p=P)

    with ExitStack() as ctx:
        if MANUAL:
            ctx.enter_context(tc.manual_schedule())
        const = ctx.enter_context(tc.tile_pool(name="const", bufs=1))
        gpool = ctx.enter_context(tc.tile_pool(name="gpool", bufs=LEAD_T + 2))
        spool = ctx.enter_context(tc.tile_pool(name="spool", bufs=4))
        rpool = ctx.enter_context(tc.tile_pool(name="rpool", bufs=3))
        psx = ctx.enter_context(tc.psum_pool(name="psx", bufs=2))
        psp = ctx.enter_context(tc.psum_pool(name="psp", bufs=3))

        w_sb = const.tile([P, 8 * CIN], BF16, name="w_sb")
        w_sb3 = w_sb[:].rearrange("p (a k) -> p a k", a=8)
        def load_w(q):
            nc.sync.dma_start(out=w_sb3[:, 2 * q:2 * q + 2, :], in_=w_v[:, 2 * q:2 * q + 2, :])

        gate_sb = const.tile([P, NT * E], BF16, name="gate_sb")
        nc.scalar.dma_start(out=gate_sb[:], in_=g_v)
        xs = []
        for g in range(NG):
            x_t = const.tile([P, GT * CIN], BF16, name="x%d" % g)
            xs.append(x_t)
        half = GT * CIN // 2
        load_w(0)
        load_w(1)
        nc.sync.dma_start(out=xs[0][:, 0:half], in_=x_v[:, 0:half])
        load_w(2)
        load_w(3)
        nc.sync.dma_start(out=xs[0][:, half:2 * half], in_=x_v[:, half:2 * half])
        for g in range(1, NG):
            nc.sync.dma_start(out=xs[g][:], in_=x_v[:, g * GT * CIN:(g + 1) * GT * CIN])

        ident = const.tile([P, P], F32, name="ident")
        make_identity(nc, ident[:])
        zero = const.tile([P, 1], F32, name="zero")
        nc.vector.memset(zero[:], 0.0)
        warm = const.tile([P, 1], F32, name="warm")
        nc.scalar.activation(out=warm[:], in_=zero[:], func=ACT.Sin)
        gs = const.tile([P, NT * E], F32, name="gs")
        nc.vector.tensor_scalar(out=gs[:], in0=gate_sb[:], scalar1=30.0 / (2.0 * math.pi),
                                scalar2=None, op0=ALU.mult)

        def copy_out(eng, dst, src):
            if eng == "s":
                nc.scalar.copy(out=dst, in_=src)
            else:
                nc.vector.tensor_copy(out=dst, in_=src)

        def transposes(bank, src_f32, first):
            for jj in range(2):
                for u in range(2):
                    c = (first + jj) * 256 + u * P
                    nc.tensor.transpose(bank[:, (jj * 2 + u) * P:(jj * 2 + u + 1) * P],
                                        src_f32[:, c:c + P], ident[:])

        def regroup(eng, grp_f32, h, bank):
            copy_out(eng,
                     grp_f32[:, h * 512:(h + 1) * 512].rearrange("p (j m u) -> p j m u", j=2, u=2),
                     bank[:].rearrange("p (j u m) -> p j m u", j=2, u=2))

        w_f32 = w_sb[:].bitcast(F32)
        w_grp = const.tile([P, 8 * CIN], BF16, name="w_grp", align_bytes=64)
        w_grp_f32 = w_grp[:].bitcast(F32)
        w_codes = const.tile([P, E * COUT], U32, name="w_codes", align_bytes=64)
        w_scl = const.tile([P, E * COUT], U8, name="w_scl", align_bytes=64)
        for q in range(4):
            wt = psp.tile([P, 512], F32, tag=("pa" if q % 2 == 0 else "pb"), name="wt%d" % q)
            transposes(wt, w_f32, 2 * q)
            regroup("s" if q % 2 == 0 else "v", w_grp_f32, q, wt)
            if q % 2 == 1:
                h = q // 2
                nc.vector.quantize_mx(out=w_codes[:, h * 512:(h + 1) * 512].bitcast(FP8X4),
                                      scales=w_scl[:, h * 512:(h + 1) * 512],
                                      in_=w_grp[:, h * 2048:(h + 1) * 2048])

        grp = {}
        banks = {}
        codes = {}
        scl = {}
        u_t = {}
        o_t = {}
        k_t = {}
        r_t = {}

        def stage_t(g):
            grp[g] = gpool.tile([P, GT * CIN], BF16, tag="grp", name="grp%d" % g, align_bytes=64)
            xf = xs[g][:].bitcast(F32)
            for h in range(2):
                bank = psx.tile([P, 512], F32, tag="xt", name="xt%d_%d" % (g, h))
                transposes(bank, xf, 2 * h)
                banks[(g, h)] = bank

        def stage_exit(g, h):
            regroup(EXIT_ENG[h], grp[g][:].bitcast(F32), h, banks[(g, h)])

        def stage_q(g):
            codes[g] = gpool.tile([P, GT * P], U32, tag="codes", name="codes%d" % g, align_bytes=64)
            scl[g] = gpool.tile([P, GT * P], U8, tag="scl", name="scl%d" % g, align_bytes=64)
            cuts = ((0, 2), (2, 4)) if g == 0 else ((0, 4),)
            for lo, hi in cuts:
                nc.vector.quantize_mx(out=codes[g][:, lo * P:hi * P].bitcast(FP8X4),
                                      scales=scl[g][:, lo * P:hi * P],
                                      in_=grp[g][:, lo * CIN:hi * CIN])

        def stage_m(g, jj):
            if jj == 0:
                u_t[g] = rpool.tile([P, GT * COUT], F32, tag="u", name="u%d" % g)
            j = g * GT + jj
            pa = psp.tile([P, 512], F32, tag="pa", name="pa%d" % j)
            pb = psp.tile([P, 512], F32, tag="pb", name="pb%d" % j)
            for h, bank in ((0, pa), (1, pb)):
                nc.tensor.matmul_mx(out=bank[:],
                                    lhsT=codes[g][:, jj * P:(jj + 1) * P].bitcast(FP8X4),
                                    lhsT_scale=scl[g][:, jj * P:(jj + 1) * P],
                                    rhs=w_codes[:, h * 512:(h + 1) * 512].bitcast(FP8X4),
                                    rhs_scale=w_scl[:, h * 512:(h + 1) * 512],
                                    start=True, stop=True)

            def gcol(t):
                return gs[:, j * E + t:j * E + t + 1]

            def stt(dst, src, t, add):
                nc.vector.scalar_tensor_tensor(out=dst, in0=src, scalar=gcol(t), in1=add,
                                               op0=ALU.mult, op1=ALU.add)

            u_dst = u_t[g][:, jj * COUT:(jj + 1) * COUT]
            sa0 = spool.tile([P, COUT], F32, tag="sa0", name="sa0_%d" % j)
            nc.scalar.activation(out=sa0[:], in_=pa[:, 0:COUT], func=ACT.Copy, scale=gcol(0))
            acc = spool.tile([P, COUT], F32, tag="acc", name="acc%d" % j)
            if TWO[jj]:
                sa1 = spool.tile([P, COUT], F32, tag="sa1", name="sa1_%d" % j)
                nc.scalar.activation(out=sa1[:], in_=pa[:, COUT:2 * COUT], func=ACT.Copy, scale=gcol(1))
                a01 = spool.tile([P, COUT], F32, tag="a01", name="a01_%d" % j)
                nc.gpsimd.tensor_tensor(out=a01[:], in0=sa0[:], in1=sa1[:], op=ALU.add)
                stt(acc[:], pb[:, 0:COUT], 2, a01[:])
            else:
                acc1 = spool.tile([P, COUT], F32, tag="acc1", name="acc1_%d" % j)
                stt(acc1[:], pa[:, COUT:2 * COUT], 1, sa0[:])
                stt(acc[:], pb[:, 0:COUT], 2, acc1[:])
            stt(u_dst, pb[:, COUT:2 * COUT], 3, acc[:])

        def width(g):
            return GT * COUT if g < WIDE_UNTIL else GT * COUT // 2

        def stage_cast(g, h):
            rw = width(g)
            k_t[(g, h)] = rpool.tile([P, rw], I32, tag="k", name="k%d_%d" % (g, h))
            src = u_t[g][:, h * rw:(h + 1) * rw]
            if CAST_ENG == "g":
                nc.gpsimd.tensor_scalar(out=k_t[(g, h)][:], in0=src, scalar1=1.0, scalar2=0.0,
                                        op0=ALU.mult, op1=ALU.add)
            else:
                nc.vector.tensor_copy(out=k_t[(g, h)][:], in_=src)

        def stage_sub(g, h):
            rw = width(g)
            r_t[(g, h)] = rpool.tile([P, rw], F32, tag="r", name="r%d_%d" % (g, h))
            nc.vector.tensor_tensor(out=r_t[(g, h)][:], in0=u_t[g][:, h * rw:(h + 1) * rw],
                                    in1=k_t[(g, h)][:], op=ALU.subtract)

        def stage_sin(g, h):
            if h == 0:
                o_t[g] = rpool.tile([P, GT * COUT], F32, tag="o", name="o%d" % g)
            rw = width(g)
            nc.scalar.activation(out=o_t[g][:, h * rw:(h + 1) * rw], in_=r_t[(g, h)][:],
                                 func=ACT.Sin, scale=2.0 * math.pi)
            if (h + 1) * rw == GT * COUT:
                nc.sync.dma_start(out=o_v[:, g * GT * COUT:(g + 1) * GT * COUT], in_=o_t[g][:])

        def tail_piece(g, lo, hi):
            kk = rpool.tile([P, 256], I32, tag="kk", name="kk%d" % lo)
            rr = rpool.tile([P, 256], F32, tag="rr", name="rr%d" % lo)
            oo = rpool.tile([P, 256], F32, tag="oo", name="oo%d" % lo)
            nc.vector.tensor_copy(out=kk[:], in_=u_t[g][:, lo:hi])
            nc.vector.tensor_tensor(out=rr[:], in0=u_t[g][:, lo:hi], in1=kk[:], op=ALU.subtract)
            nc.scalar.activation(out=oo[:], in_=rr[:], func=ACT.Sin, scale=2.0 * math.pi)
            nc.sync.dma_start(out=o_v[:, g * GT * COUT + lo:g * GT * COUT + hi], in_=oo[:])

        for i in range(-LEAD_T, NG + 1):
            tg, qg, mg, rg = i + LEAD_T, i + LEAD_Q, i, i - 1
            has_t = tg < NG
            has_q = 0 <= qg < NG
            has_m = 0 <= mg < NG
            has_r = 0 <= rg < NG - 1
            if has_t:
                stage_t(tg)
            for s in range(GT):
                if has_r and s == 0:
                    stage_cast(rg, 0)
                if has_m:
                    stage_m(mg, s)
                    if mg == NG - 1:
                        tail_piece(mg, s * COUT, (s + 1) * COUT)
                two_pieces = has_r and rg >= WIDE_UNTIL
                if two_pieces and s == 1:
                    stage_cast(rg, 1)
                if two_pieces and s == 0:
                    stage_sub(rg, 0)
                if has_q and s == 1:
                    stage_q(qg)
                if has_r and s == 2:
                    stage_sub(rg, 1 if two_pieces else 0)
                if has_t and s < 2:
                    stage_exit(tg, s)
                if two_pieces and s == 2:
                    stage_sin(rg, 0)
                if has_r and s == 3:
                    stage_sin(rg, 1 if two_pieces else 0)
